import numpy as np
import ml_dtypes


def mxq(x, axis, fmt="e4m3"):
    dtype, down = {"e4m3": (ml_dtypes.float8_e4m3fn, 7), "e5m2": (ml_dtypes.float8_e5m2, 14)}[fmt]
    v = np.moveaxis(np.asarray(x, np.float32).astype(ml_dtypes.bfloat16).astype(np.float64), axis, -1)
    blocks = v.reshape(v.shape[:-1] + (-1, 32))
    amax = np.abs(blocks).max(-1, keepdims=True)
    byte = np.maximum(np.where(amax > 0, np.frexp(amax)[1] - 1 + 127, 0) - down, 1)
    scale = np.exp2(byte - 127.0)
    codes = (blocks / scale).astype(np.float32).astype(dtype).astype(np.float64)
    return np.moveaxis((codes * scale).reshape(v.shape), -1, axis)


WIDE = False


def mx_kscale(k):
    if not WIDE:
        return np.ones(k)
    levels = np.array([10, -10, 5, -5, 0])
    a = np.random.permutation(np.resize(levels, k // 512 * 4)).reshape(k // 512, 4)
    idx = np.arange(k)
    return np.exp2(a[idx // 512, idx % 128 // 32])


BF16 = ml_dtypes.bfloat16


def bf(x):
    return np.asarray(x, np.float32).astype(BF16)


def f64(x):
    return np.asarray(x).astype(np.float64)


B, N1, N2, D, H, DH = 4, 1536, 512, 512, 4, 64
E = H * DH


def rope_tables(n, d):
    inv = 1.0 / (10000.0 ** (np.arange(0, d, 2) / d))
    ang = np.outer(np.arange(n), inv)
    return np.repeat(np.cos(ang), 2, axis=-1), np.repeat(np.sin(ang), 2, axis=-1)


def apply_rope(x, cos, sin):
    xr = x.reshape(x.shape[:-1] + (-1, 2))
    x_real, x_imag = xr[..., 0], xr[..., 1]
    x_rot = np.stack([-x_imag, x_real], axis=-1).reshape(x.shape)
    return x * cos[None, None] + x_rot * sin[None, None]


def split_heads(t):
    b, n, _ = t.shape
    return t.reshape(b, n, H, DH).transpose(0, 2, 1, 3)


def setup_inputs():
    s1, s2 = mx_kscale(D), mx_kscale(D)
    cos1, sin1 = rope_tables(N1, DH)
    cos2, sin2 = rope_tables(N2, DH)

    def w(s):
        return bf(np.random.standard_normal((D, E)) * 1.4 / np.sqrt(D) / s[:, None])

    def b():
        return bf(np.random.standard_normal(E) * 0.3)

    return {"x_1": bf(np.random.standard_normal((B, N1, D)) * s1), "x_2": bf(np.random.standard_normal((B, N2, D)) * s2),
            "cos1": bf(cos1), "sin1": bf(sin1), "cos2": bf(cos2), "sin2": bf(sin2),
            "wq1": w(s1), "bq1": b(), "wk1": w(s1), "bk1": b(),
            "wq2": w(s2), "bq2": b(), "wk2": w(s2), "bk2": b()}


def reference(x_1, x_2, cos1, sin1, cos2, sin2, wq1, bq1, wk1, bk1, wq2, bq2, wk2, bk2):
    x1q = mxq(f64(x_1), 2, "e4m3")
    x2q = mxq(f64(x_2), 2, "e4m3")
    q = np.concatenate([(x1q @ mxq(f64(wq1), 0, "e4m3")) + f64(bq1),
                        (x2q @ mxq(f64(wq2), 0, "e4m3")) + f64(bq2)], axis=1)
    k = np.concatenate([(x1q @ mxq(f64(wk1), 0, "e4m3")) + f64(bk1),
                        (x2q @ mxq(f64(wk2), 0, "e4m3")) + f64(bk2)], axis=1)
    q, k = split_heads(q), split_heads(k)
    q = q * (DH ** -0.5)
    cos = np.concatenate([f64(cos1), f64(cos2)], axis=0)
    sin = np.concatenate([f64(sin1), f64(sin2)], axis=0)
    return apply_rope(q, cos, sin), apply_rope(k, cos, sin)

@@ -1,0 +1,231 @@
+from contextlib import ExitStack
+
+import concourse.mybir as mybir
+from concourse.masks import make_identity
+
+F32 = mybir.dt.float32
+BF16 = mybir.dt.bfloat16
+U32 = mybir.dt.uint32
+U8 = mybir.dt.uint8
+FP8X4 = mybir.dt.float8_e4m3fn_x4
+ALU = mybir.AluOpType
+ACT = mybir.ActivationFunctionType
+
+P = 128
+B, N1, N2, D, H, DH = 4, 1536, 512, 512, 4, 64
+E = H * DH
+FLOPS = 2 * B * (N1 + N2) * D * 2 * E
+
+ROUNDS = [(0, tg, b) for tg in range(3) for b in range(B)] + [(1, 0, b) for b in range(B)]
+NR = len(ROUNDS)
+MANUAL = True
+GT = 2
+
+
+def tile_dualmultiheadattention_pa_t_kernel(tc, x_1, x_2, cos1, sin1, cos2, sin2, wq1, bq1, wk1, bk1, wq2, bq2, wk2, bk2, out_0, out_1):
+    nc = tc.nc
+    with ExitStack() as ctx:
+        if MANUAL:
+            ctx.enter_context(tc.manual_schedule())
+        const = ctx.enter_context(tc.tile_pool(name="const", bufs=1))
+        xpool = ctx.enter_context(tc.tile_pool(name="xin", bufs=NR))
+        gpool = ctx.enter_context(tc.tile_pool(name="grouped", bufs=3))
+        cpool = ctx.enter_context(tc.tile_pool(name="codes", bufs=3))
+        tpool = ctx.enter_context(tc.tile_pool(name="proj", bufs=8))
+        rpool = ctx.enter_context(tc.tile_pool(name="prod", bufs=2))
+        ypool = ctx.enter_context(tc.tile_pool(name="res", bufs=3))
+        ps_xt = ctx.enter_context(tc.psum_pool(name="ps_xt", bufs=2))
+        ps_p1 = ctx.enter_context(tc.psum_pool(name="ps_p1", bufs=3))
+        ps_p2 = ctx.enter_context(tc.psum_pool(name="ps_p2", bufs=3))
+
+        def x_view(r):
+            s, tg, b = ROUNDS[r]
+            if s == 0:
+                return x_1[b].rearrange("(p t) k -> p t k", t=12)[:, 4 * tg : 4 * tg + 4, :]
+            return x_2[b].rearrange("(p t) k -> p t k", t=4)
+
+        def out_view(o, r):
+            s, tg, b = ROUNDS[r]
+            if s == 0:
+                return o[b, :, 0:N1, :].rearrange("h (p t) c -> p h t c", t=12)[:, :, 4 * tg : 4 * tg + 4, :]
+            return o[b, :, N1 : N1 + N2, :].rearrange("h (p t) c -> p h t c", t=4)
+
+        xs = []
+
+        def load_x(r):
+            x_sb = xpool.tile([P, 4 * D], BF16, name="x_sb")
+            nc.sync.dma_start(out=x_sb[:].rearrange("p (t k) -> p t k", t=4), in_=x_view(r))
+            xs.append(x_sb)
+
+        ident = const.tile([P, P], F32, name="ident")
+        make_identity(nc, ident[:])
+        brow = const.tile([P, P], BF16, name="brow")
+        nc.vector.memset(brow[:], 0.0)
+
+        wraw = [const.tile([P, 2, 4, E], BF16, name="wraw%d" % s) for s in range(2)]
+        wgrp = [const.tile([P, 2 * E, 4], BF16, name="wgrp%d" % s, align_bytes=64) for s in range(2)]
+        wcod = [const.tile([P, 2 * E], U32, name="wcod%d" % s, align_bytes=64) for s in range(2)]
+        wscl = [const.tile([P, 2 * E], U8, name="wscl%d" % s, align_bytes=64) for s in range(2)]
+        craw = const.tile([P, 16, DH], BF16, name="craw")
+        sraw = const.tile([P, 16, DH], BF16, name="sraw")
+        tab = const.tile([P, 16, 2 * DH], BF16, name="tab")
+
+        def load_w(eng, s, k, w):
+            eng.dma_start(
+                out=wraw[s][:, k].rearrange("q (u e) c -> q u (e c)", u=2),
+                in_=w.rearrange("(u q e) c -> q u (e c)", u=2, e=2),
+            )
+
+        load_x(0)
+        load_w(nc.scalar, 0, 0, wq1)
+        load_w(nc.scalar, 0, 1, wk1)
+        for r0, bvec in ((0, bq1), (2, bk1), (4, bq2), (6, bk2)):
+            nc.sync.dma_start(out=brow[r0 : r0 + 2, :], in_=bvec.rearrange("(r m) -> r m", r=2))
+        nc.scalar.dma_start(out=craw[:, 0:12, :], in_=cos1.rearrange("(p t) c -> p t c", t=12))
+        nc.scalar.dma_start(out=sraw[:, 0:12, :], in_=sin1.rearrange("(p t) c -> p t c", t=12))
+        for r in range(1, 6):
+            load_x(r)
+        nc.sync.dma_start(out=craw[:, 12:16, :], in_=cos2.rearrange("(p t) c -> p t c", t=4))
+        nc.sync.dma_start(out=sraw[:, 12:16, :], in_=sin2.rearrange("(p t) c -> p t c", t=4))
+        load_w(nc.sync, 1, 0, wq2)
+        load_w(nc.sync, 1, 1, wk2)
+        for r in range(6, NR):
+            load_x(r)
+
+        def regroup_w(copy, s, k):
+            copy(
+                out=wgrp[s][:, k * E : (k + 1) * E, :].rearrange("p (c i) t -> p c t i", i=4),
+                in_=wraw[s][:, k].rearrange("p t (c i) -> p c t i", i=4),
+            )
+
+        def quantise_w(s):
+            nc.vector.quantize_mx(
+                out=wcod[s][:].bitcast(FP8X4), scales=wscl[s][:], in_=wgrp[s][:].rearrange("p c t -> p (c t)")
+            )
+
+        tabv = tab[:].rearrange("p t (j i e) -> p t j i e", i=2, e=2)
+        crv = craw[:].rearrange("p t (j e) -> p t j e", e=2)
+        srv = sraw[:].rearrange("p t (j e) -> p t j e", e=2)
+
+        def table_op(on_vector, g, k):
+            tsl = slice(4 * g, 4 * g + 4)
+            src, i, e, sign = ((crv, 0, 0, 1.0), (srv, 0, 1, -1.0), (srv, 1, 0, 1.0), (crv, 1, 1, 1.0))[k]
+            dst = tabv[:, tsl, :, i, e]
+            val = src[:, tsl, :, i]
+            if on_vector:
+                nc.vector.tensor_scalar_mul(out=dst, in0=val, scalar1=sign)
+            else:
+                nc.scalar.mul(out=dst, in_=val, mul=sign)
+
+        grouped = {}
+        xcod = {}
+        xscl = {}
+
+        def transpose_x(r):
+            words = xs[r][:].bitcast(F32)
+            grp = gpool.tile([P, 8 * P], F32, name="grp", align_bytes=64)
+            for half in range(2):
+                xt = ps_xt.tile([P, 2, 2, P], F32, name="xt")
+                for a in range(2):
+                    for u in range(2):
+                        c0 = (2 * half + a) * 256 + u * P
+                        nc.tensor.transpose(xt[:, a, u, :], words[:, c0 : c0 + P], ident[:])
+                nc.scalar.copy(
+                    out=grp[:, half * 512 : (half + 1) * 512].rearrange("q (a p u) -> q a p u", a=2, u=2),
+                    in_=xt[:].rearrange("q a u p -> q a p u"),
+                )
+            grouped[r] = grp
+
+        def quantise_x(r):
+            cod = cpool.tile([P, 4 * P], U32, name="xcod", align_bytes=64)
+            scl = cpool.tile([P, 4 * P], U8, name="xscl", align_bytes=64)
+            nc.vector.quantize_mx(out=cod[:].bitcast(FP8X4), scales=scl[:], in_=grouped[r][:].bitcast(BF16))
+            xcod[r] = cod
+            xscl[r] = scl
+
+        def project(r):
+            s = ROUNDS[r][0]
+            ts = []
+            for fb in range(4):
+                fsl = slice(fb * P, (fb + 1) * P)
+                p1 = ps_p1.tile([P, 4 * P], F32, name="p1")
+                nc.tensor.matmul_mx(
+                    out=p1[:],
+                    lhsT=wcod[s][:, fsl].bitcast(FP8X4),
+                    lhsT_scale=wscl[s][:, fsl],
+                    rhs=xcod[r][:].bitcast(FP8X4),
+                    rhs_scale=xscl[r][:],
+                    start=True,
+                    stop=True,
+                )
+                t_sb = tpool.tile([P, 4 * P], F32, name="t_sb")
+                nc.scalar.activation(
+                    out=t_sb[:],
+                    in_=p1[:],
+                    func=ACT.Identity,
+                    bias=bias_p[:, 4 * s + fb : 4 * s + fb + 1],
+                    scale=(0.125 if fb < 2 else 1.0),
+                )
+                ts.append(t_sb)
+            return ts
+
+        regroup_w(nc.vector.tensor_copy, 0, 0)
+        regroup_w(nc.vector.tensor_copy, 0, 1)
+        quantise_w(0)
+        transpose_x(0)
+        brow32 = const.tile([P, P], F32, name="brow32")
+        nc.vector.tensor_copy(out=brow32[:], in_=brow[:])
+        bT = ps_xt.tile([P, 2, 2, P], F32, name="xt")
+        nc.tensor.transpose(bT[:, 0, 0, :], brow32[:], ident[:])
+        quantise_x(0)
+        bias_p = const.tile([P, 8], F32, name="bias_p")
+        bv = bias_p[:].rearrange("p (s k r) -> p s k r", s=2, k=2)
+        tv = bT[:, 0, 0, 0:8].rearrange("p (s k r) -> p s k r", s=2, k=2)
+        nc.vector.tensor_scalar_mul(out=bv[:, :, 0, :], in0=tv[:, :, 0, :], scalar1=0.125)
+        nc.vector.tensor_copy(out=bv[:, :, 1, :], in_=tv[:, :, 1, :])
+        for k in range(4):
+            table_op(True, 0, k)
+        transpose_x(1)
+
+        for r in range(NR):
+            s, tg, b = ROUNDS[r]
+            g = tg if s == 0 else 3
+            ts = project(r)
+            if r + 2 < NR:
+                transpose_x(r + 2)
+            if r < 12:
+                table_op(False, r // 4 + 1, r % 4)
+            if r in (4, 5):
+                regroup_w(nc.scalar.copy, 1, r - 4)
+            prod = rpool.tile([P, 4, 8 * P], F32, name="prod")
+            y = ypool.tile([P, 2 * H, 4, DH], F32, name="y")
+            for tau in range(4):
+                p2 = ps_p2.tile([P, 4 * P], F32, name="p2")
+                for fb in range(4):
+                    nc.tensor.transpose(p2[:, fb * P : (fb + 1) * P], ts[fb][:, tau * P : (tau + 1) * P], ident[:])
+                nc.vector.tensor_tensor(
+                    out=prod[:, tau, :].rearrange("p (g j i e) -> p g j i e", g=8, i=2, e=2),
+                    in0=p2[:].rearrange("p (g j e) -> p g j e", g=8, e=2).unsqueeze(3).to_broadcast([P, 8, 32, 2, 2]),
+                    in1=tab[:, 4 * g + tau, :]
+                    .rearrange("p (j i e) -> p j i e", i=2, e=2)
+                    .unsqueeze(1)
+                    .to_broadcast([P, 8, 32, 2, 2]),
+                    op=ALU.mult,
+                )
+                if r == 0 and tau == 0:
+                    quantise_x(1)
+                if tau == 1 and r + 2 < NR:
+                    quantise_x(r + 2)
+                if tau == 2 and r == 7:
+                    quantise_w(1)
+                if tau % GT == GT - 1:
+                    t0 = tau - GT + 1
+                    pv = prod[:, t0 : tau + 1, :].rearrange("p t (g c e) -> p t g c e", g=8, e=2)
+                    nc.gpsimd.tensor_tensor(
+                        out=y[:].rearrange("p g t c -> p t g c")[:, t0 : tau + 1],
+                        in0=pv[:, :, :, :, 0],
+                        in1=pv[:, :, :, :, 1],
+                        op=ALU.add,
+                    )
+            nc.sync.dma_start(out=out_view(out_0, r), in_=y[:, 0:H])
+            nc.sync.dma_start(out=out_view(out_1, r), in_=y[:, H : 2 * H])

@@ -18,25 +18,24 @@ FLOPS = 2 * B * (N1 + N2) * D * 2 * E
 
 ROUNDS = [(0, tg, b) for tg in range(3) for b in range(B)] + [(1, 0, b) for b in range(B)]
 NR = len(ROUNDS)
-MANUAL = True
-GT = 2
+POOL_BLOCKS = ()
 
 
 def tile_dualmultiheadattention_pa_t_kernel(tc, x_1, x_2, cos1, sin1, cos2, sin2, wq1, bq1, wk1, bk1, wq2, bq2, wk2, bk2, out_0, out_1):
     nc = tc.nc
     with ExitStack() as ctx:
-        if MANUAL:
-            ctx.enter_context(tc.manual_schedule())
+        ctx.enter_context(tc.manual_schedule())
         const = ctx.enter_context(tc.tile_pool(name="const", bufs=1))
         xpool = ctx.enter_context(tc.tile_pool(name="xin", bufs=NR))
         gpool = ctx.enter_context(tc.tile_pool(name="grouped", bufs=3))
         cpool = ctx.enter_context(tc.tile_pool(name="codes", bufs=3))
-        tpool = ctx.enter_context(tc.tile_pool(name="proj", bufs=8))
-        rpool = ctx.enter_context(tc.tile_pool(name="prod", bufs=2))
+        spool = ctx.enter_context(tc.tile_pool(name="tabsrc", bufs=2))
+        tpool = None
+        rpool = ctx.enter_context(tc.tile_pool(name="prod", bufs=4))
         ypool = ctx.enter_context(tc.tile_pool(name="res", bufs=3))
-        ps_xt = ctx.enter_context(tc.psum_pool(name="ps_xt", bufs=2))
-        ps_p1 = ctx.enter_context(tc.psum_pool(name="ps_p1", bufs=3))
-        ps_p2 = ctx.enter_context(tc.psum_pool(name="ps_p2", bufs=3))
+        ps_xt = ctx.enter_context(tc.psum_pool(name="ps_xt", bufs=1))
+        ps_p1 = ctx.enter_context(tc.psum_pool(name="ps_p1", bufs=5))
+        ps_p2 = ctx.enter_context(tc.psum_pool(name="ps_p2", bufs=2))
 
         def x_view(r):
             s, tg, b = ROUNDS[r]
@@ -68,7 +67,7 @@ def tile_dualmultiheadattention_pa_t_kernel(tc, x_1, x_2, cos1, sin1, cos2, sin2
         wscl = [const.tile([P, 2 * E], U8, name="wscl%d" % s, align_bytes=64) for s in range(2)]
         craw = const.tile([P, 16, DH], BF16, name="craw")
         sraw = const.tile([P, 16, DH], BF16, name="sraw")
-        tab = const.tile([P, 16, 2 * DH], BF16, name="tab")
+        dtab = const.tile([P, 2, 16 * P], F32, name="dtab")
 
         def load_w(eng, s, k, w):
             eng.dma_start(
@@ -76,14 +75,20 @@ def tile_dualmultiheadattention_pa_t_kernel(tc, x_1, x_2, cos1, sin1, cos2, sin2
                 in_=w.rearrange("(u q e) c -> q u (e c)", u=2, e=2),
             )
 
+        cos1v = cos1.rearrange("(p t) c -> p t c", t=12)
+        sin1v = sin1.rearrange("(p t) c -> p t c", t=12)
         load_x(0)
+        nc.scalar.dma_start(out=craw[:, 0:4, :], in_=cos1v[:, 0:4, :])
+        nc.scalar.dma_start(out=sraw[:, 0:4, :], in_=sin1v[:, 0:4, :])
         load_w(nc.scalar, 0, 0, wq1)
         load_w(nc.scalar, 0, 1, wk1)
         for r0, bvec in ((0, bq1), (2, bk1), (4, bq2), (6, bk2)):
             nc.sync.dma_start(out=brow[r0 : r0 + 2, :], in_=bvec.rearrange("(r m) -> r m", r=2))
-        nc.scalar.dma_start(out=craw[:, 0:12, :], in_=cos1.rearrange("(p t) c -> p t c", t=12))
-        nc.scalar.dma_start(out=sraw[:, 0:12, :], in_=sin1.rearrange("(p t) c -> p t c", t=12))
-        for r in range(1, 6):
+        for r in range(1, 4):
+            load_x(r)
+        nc.sync.dma_start(out=craw[:, 4:12, :], in_=cos1v[:, 4:12, :])
+        nc.sync.dma_start(out=sraw[:, 4:12, :], in_=sin1v[:, 4:12, :])
+        for r in range(4, 6):
             load_x(r)
         nc.sync.dma_start(out=craw[:, 12:16, :], in_=cos2.rearrange("(p t) c -> p t c", t=4))
         nc.sync.dma_start(out=sraw[:, 12:16, :], in_=sin2.rearrange("(p t) c -> p t c", t=4))
@@ -91,6 +96,12 @@ def tile_dualmultiheadattention_pa_t_kernel(tc, x_1, x_2, cos1, sin1, cos2, sin2
         load_w(nc.sync, 1, 1, wk2)
         for r in range(6, NR):
             load_x(r)
+
+        swp = const.tile([P, P], F32, name="swp")
+        swv = swp[:].rearrange("p (m e) -> p m e", e=2)
+        idv = ident[:].rearrange("p (m e) -> p m e", e=2)
+        nc.vector.tensor_copy(out=swv[:, :, 0], in_=idv[:, :, 1])
+        nc.vector.tensor_copy(out=swv[:, :, 1], in_=idv[:, :, 0])
 
         def regroup_w(copy, s, k):
             copy(
@@ -103,38 +114,50 @@ def tile_dualmultiheadattention_pa_t_kernel(tc, x_1, x_2, cos1, sin1, cos2, sin2
                 out=wcod[s][:].bitcast(FP8X4), scales=wscl[s][:], in_=wgrp[s][:].rearrange("p c t -> p (c t)")
             )
 
-        tabv = tab[:].rearrange("p t (j i e) -> p t j i e", i=2, e=2)
-        crv = craw[:].rearrange("p t (j e) -> p t j e", e=2)
         srv = sraw[:].rearrange("p t (j e) -> p t j e", e=2)
+        tabsrc = {}
 
-        def table_op(on_vector, g, k):
+        def table_sources(eng, g):
             tsl = slice(4 * g, 4 * g + 4)
-            src, i, e, sign = ((crv, 0, 0, 1.0), (srv, 0, 1, -1.0), (srv, 1, 0, 1.0), (crv, 1, 1, 1.0))[k]
-            dst = tabv[:, tsl, :, i, e]
-            val = src[:, tsl, :, i]
-            if on_vector:
-                nc.vector.tensor_scalar_mul(out=dst, in0=val, scalar1=sign)
-            else:
-                nc.scalar.mul(out=dst, in_=val, mul=sign)
+            csrc = spool.tile([P, 4, 2, DH], F32, name="csrc")
+            ssrc = spool.tile([P, 4, 2, DH], F32, name="ssrc")
+            eng.tensor_scalar(
+                out=csrc[:], in0=craw[:, tsl, :].unsqueeze(2).to_broadcast([P, 4, 2, DH]),
+                scalar1=1.0, scalar2=0.0, op0=ALU.mult, op1=ALU.add,
+            )
+            ssv = ssrc[:].rearrange("p t h (j e) -> p t h j e", e=2)
+            for e in range(2):
+                eng.tensor_scalar(
+                    out=ssv[:, :, :, :, e],
+                    in0=srv[:, tsl, :, 1 - e].unsqueeze(2).to_broadcast([P, 4, 2, DH // 2]),
+                    scalar1=(1.0 if e == 0 else -1.0), scalar2=0.0, op0=ALU.mult, op1=ALU.add,
+                )
+            tabsrc[g] = (csrc, ssrc)
+
+        def table_transpose(pool, name, g, z):
+            bank = pool.tile([P, 4, P], F32, name=name)
+            for t in range(4):
+                nc.tensor.transpose(bank[:, t, :], tabsrc[g][z][:, t].rearrange("p h c -> p (h c)"), ident[:])
+            nc.scalar.copy(out=dtab[:, z, 4 * g * P : 4 * (g + 1) * P], in_=bank[:].rearrange("p t n -> p (t n)"))
 
         grouped = {}
         xcod = {}
         xscl = {}
 
-        def transpose_x(r):
+        def transpose_x(r, half):
             words = xs[r][:].bitcast(F32)
-            grp = gpool.tile([P, 8 * P], F32, name="grp", align_bytes=64)
-            for half in range(2):
-                xt = ps_xt.tile([P, 2, 2, P], F32, name="xt")
-                for a in range(2):
-                    for u in range(2):
-                        c0 = (2 * half + a) * 256 + u * P
-                        nc.tensor.transpose(xt[:, a, u, :], words[:, c0 : c0 + P], ident[:])
-                nc.scalar.copy(
-                    out=grp[:, half * 512 : (half + 1) * 512].rearrange("q (a p u) -> q a p u", a=2, u=2),
-                    in_=xt[:].rearrange("q a u p -> q a p u"),
-                )
-            grouped[r] = grp
+            if half == 0:
+                grp = gpool.tile([P, 8 * P], F32, name="grp", align_bytes=64)
+                grouped[r] = grp
+            xt = ps_xt.tile([P, 2, 2, P], F32, name="xt")
+            for a in range(2):
+                for u in range(2):
+                    c0 = (2 * half + a) * 256 + u * P
+                    nc.tensor.transpose(xt[:, a, u, :], words[:, c0 : c0 + P], ident[:])
+            nc.scalar.copy(
+                out=grouped[r][:, half * 512 : (half + 1) * 512].rearrange("q (a p u) -> q a p u", a=2, u=2),
+                in_=xt[:].rearrange("q a u p -> q a p u"),
+            )
 
         def quantise_x(r):
             cod = cpool.tile([P, 4 * P], U32, name="xcod", align_bytes=64)
@@ -143,9 +166,10 @@ def tile_dualmultiheadattention_pa_t_kernel(tc, x_1, x_2, cos1, sin1, cos2, sin2
             xcod[r] = cod
             xscl[r] = scl
 
+        banks = {}
+
         def project(r):
             s = ROUNDS[r][0]
-            ts = []
             for fb in range(4):
                 fsl = slice(fb * P, (fb + 1) * P)
                 p1 = ps_p1.tile([P, 4 * P], F32, name="p1")
@@ -158,74 +182,84 @@ def tile_dualmultiheadattention_pa_t_kernel(tc, x_1, x_2, cos1, sin1, cos2, sin2
                     start=True,
                     stop=True,
                 )
-                t_sb = tpool.tile([P, 4 * P], F32, name="t_sb")
-                nc.scalar.activation(
-                    out=t_sb[:],
-                    in_=p1[:],
-                    func=ACT.Identity,
-                    bias=bias_p[:, 4 * s + fb : 4 * s + fb + 1],
-                    scale=(0.125 if fb < 2 else 1.0),
-                )
-                ts.append(t_sb)
-            return ts
+                banks[(r, fb)] = p1
 
+        table_sources(nc.vector, 0)
         regroup_w(nc.vector.tensor_copy, 0, 0)
         regroup_w(nc.vector.tensor_copy, 0, 1)
         quantise_w(0)
-        transpose_x(0)
+        transpose_x(0, 0)
+        table_transpose(ps_p2, "p2", 0, 0)
+        transpose_x(0, 1)
+        table_transpose(ps_p2, "p2", 0, 1)
+        quantise_x(0)
+        transpose_x(1, 0)
+        transpose_x(1, 1)
+        project(0)
         brow32 = const.tile([P, P], F32, name="brow32")
         nc.vector.tensor_copy(out=brow32[:], in_=brow[:])
-        bT = ps_xt.tile([P, 2, 2, P], F32, name="xt")
-        nc.tensor.transpose(bT[:, 0, 0, :], brow32[:], ident[:])
-        quantise_x(0)
+        bT = ps_p1.tile([P, 4 * P], F32, name="p1")
+        nc.tensor.transpose(bT[:, 0:P], brow32[:], ident[:])
         bias_p = const.tile([P, 8], F32, name="bias_p")
-        bv = bias_p[:].rearrange("p (s k r) -> p s k r", s=2, k=2)
-        tv = bT[:, 0, 0, 0:8].rearrange("p (s k r) -> p s k r", s=2, k=2)
-        nc.vector.tensor_scalar_mul(out=bv[:, :, 0, :], in0=tv[:, :, 0, :], scalar1=0.125)
-        nc.vector.tensor_copy(out=bv[:, :, 1, :], in_=tv[:, :, 1, :])
-        for k in range(4):
-            table_op(True, 0, k)
-        transpose_x(1)
+        nc.vector.tensor_copy(out=bias_p[:], in_=bT[:, 0:8])
+        transpose_x(2, 0)
+        transpose_x(2, 1)
 
         for r in range(NR):
             s, tg, b = ROUNDS[r]
             g = tg if s == 0 else 3
-            ts = project(r)
-            if r + 2 < NR:
-                transpose_x(r + 2)
-            if r < 12:
-                table_op(False, r // 4 + 1, r % 4)
-            if r in (4, 5):
-                regroup_w(nc.scalar.copy, 1, r - 4)
-            prod = rpool.tile([P, 4, 8 * P], F32, name="prod")
             y = ypool.tile([P, 2 * H, 4, DH], F32, name="y")
-            for tau in range(4):
-                p2 = ps_p2.tile([P, 4 * P], F32, name="p2")
-                for fb in range(4):
-                    nc.tensor.transpose(p2[:, fb * P : (fb + 1) * P], ts[fb][:, tau * P : (tau + 1) * P], ident[:])
-                nc.vector.tensor_tensor(
-                    out=prod[:, tau, :].rearrange("p (g j i e) -> p g j i e", g=8, i=2, e=2),
-                    in0=p2[:].rearrange("p (g j e) -> p g j e", g=8, e=2).unsqueeze(3).to_broadcast([P, 8, 32, 2, 2]),
-                    in1=tab[:, 4 * g + tau, :]
-                    .rearrange("p (j i e) -> p j i e", i=2, e=2)
-                    .unsqueeze(1)
-                    .to_broadcast([P, 8, 32, 2, 2]),
-                    op=ALU.mult,
-                )
-                if r == 0 and tau == 0:
-                    quantise_x(1)
-                if tau == 1 and r + 2 < NR:
-                    quantise_x(r + 2)
-                if tau == 2 and r == 7:
-                    quantise_w(1)
-                if tau % GT == GT - 1:
-                    t0 = tau - GT + 1
-                    pv = prod[:, t0 : tau + 1, :].rearrange("p t (g c e) -> p t g c e", g=8, e=2)
+            if r % 4 == 0 and r < 12:
+                table_sources(nc.gpsimd, r // 4 + 1)
+            for fb in range(4):
+                p1 = banks[(r, fb)]
+                bcol = bias_p[:, 4 * s + fb : 4 * s + fb + 1]
+                dsl = dtab[:, :, 4 * g * P : 4 * (g + 1) * P]
+                prod = rpool.tile([P, 2, 4 * P], F32, name="prod")
+                if (r % 1, fb) in POOL_BLOCKS:
+                    t_sb = tpool.tile([P, 4 * P], F32, name="t_sb")
+                    nc.scalar.activation(out=t_sb[:], in_=p1[:], func=ACT.Identity, bias=bcol, scale=1.0)
                     nc.gpsimd.tensor_tensor(
-                        out=y[:].rearrange("p g t c -> p t g c")[:, t0 : tau + 1],
-                        in0=pv[:, :, :, :, 0],
-                        in1=pv[:, :, :, :, 1],
-                        op=ALU.add,
+                        out=prod[:], in0=t_sb[:].unsqueeze(1).to_broadcast([P, 2, 4 * P]), in1=dsl, op=ALU.mult
                     )
-            nc.sync.dma_start(out=out_view(out_0, r), in_=y[:, 0:H])
+                else:
+                    nc.vector.scalar_tensor_tensor(
+                        out=prod[:],
+                        in0=p1[:].unsqueeze(1).to_broadcast([P, 2, 4 * P]),
+                        scalar=bcol,
+                        in1=dsl,
+                        op0=ALU.add,
+                        op1=ALU.mult,
+                    )
+                if r == 0 and fb == 1:
+                    quantise_x(1)
+                p2 = ps_p2.tile([P, 4, P], F32, name="p2")
+                for tau in range(4):
+                    tsl = slice(tau * P, (tau + 1) * P)
+                    nc.tensor.matmul(
+                        out=p2[:, tau, :], lhsT=prod[:, 0, tsl], rhs=ident[:], is_transpose=True, start=True, stop=False
+                    )
+                    nc.tensor.matmul(
+                        out=p2[:, tau, :], lhsT=prod[:, 1, tsl], rhs=swp[:], is_transpose=True, start=False, stop=True
+                    )
+                nc.scalar.mul(
+                    out=y[:, 2 * fb : 2 * fb + 2],
+                    in_=p2[:].rearrange("p t (h c) -> p h t c", h=2),
+                    mul=(0.125 if fb < 2 else 1.0),
+                )
+                if fb < 2 and r + 3 < NR:
+                    transpose_x(r + 3, fb)
+                if fb == 1:
+                    nc.sync.dma_start(out=out_view(out_0, r), in_=y[:, 0:H])
+                if fb == 2:
+                    if r % 4 in (1, 2) and r < 12:
+                        table_transpose(ps_xt, "xt", r // 4 + 1, r % 4 - 1)
+                    if r in (4, 5):
+                        regroup_w(nc.scalar.copy, 1, r - 4)
+                    if r + 1 < NR:
+                        project(r + 1)
+            if r + 2 < NR:
+                quantise_x(r + 2)
+            if r == 7:
+                quantise_w(1)
             nc.sync.dma_start(out=out_view(out_1, r), in_=y[:, H : 2 * H])

@@ -18,24 +18,25 @@ FLOPS = 2 * B * (N1 + N2) * D * 2 * E
 
 ROUNDS = [(0, tg, b) for tg in range(3) for b in range(B)] + [(1, 0, b) for b in range(B)]
 NR = len(ROUNDS)
-POOL_BLOCKS = ()
+MANUAL = True
+GT = 2
 
 
 def tile_dualmultiheadattention_pa_t_kernel(tc, x_1, x_2, cos1, sin1, cos2, sin2, wq1, bq1, wk1, bk1, wq2, bq2, wk2, bk2, out_0, out_1):
     nc = tc.nc
     with ExitStack() as ctx:
-        ctx.enter_context(tc.manual_schedule())
+        if MANUAL:
+            ctx.enter_context(tc.manual_schedule())
         const = ctx.enter_context(tc.tile_pool(name="const", bufs=1))
         xpool = ctx.enter_context(tc.tile_pool(name="xin", bufs=NR))
         gpool = ctx.enter_context(tc.tile_pool(name="grouped", bufs=3))
         cpool = ctx.enter_context(tc.tile_pool(name="codes", bufs=3))
-        spool = ctx.enter_context(tc.tile_pool(name="tabsrc", bufs=2))
-        tpool = None
-        rpool = ctx.enter_context(tc.tile_pool(name="prod", bufs=4))
+        tpool = ctx.enter_context(tc.tile_pool(name="proj", bufs=8))
+        rpool = ctx.enter_context(tc.tile_pool(name="prod", bufs=2))
         ypool = ctx.enter_context(tc.tile_pool(name="res", bufs=3))
-        ps_xt = ctx.enter_context(tc.psum_pool(name="ps_xt", bufs=1))
-        ps_p1 = ctx.enter_context(tc.psum_pool(name="ps_p1", bufs=5))
-        ps_p2 = ctx.enter_context(tc.psum_pool(name="ps_p2", bufs=2))
+        ps_xt = ctx.enter_context(tc.psum_pool(name="ps_xt", bufs=2))
+        ps_p1 = ctx.enter_context(tc.psum_pool(name="ps_p1", bufs=2))
+        ps_p2 = ctx.enter_context(tc.psum_pool(name="ps_p2", bufs=4))
 
         def x_view(r):
             s, tg, b = ROUNDS[r]
@@ -67,7 +68,7 @@ def tile_dualmultiheadattention_pa_t_kernel(tc, x_1, x_2, cos1, sin1, cos2, sin2
         wscl = [const.tile([P, 2 * E], U8, name="wscl%d" % s, align_bytes=64) for s in range(2)]
         craw = const.tile([P, 16, DH], BF16, name="craw")
         sraw = const.tile([P, 16, DH], BF16, name="sraw")
-        dtab = const.tile([P, 2, 16 * P], F32, name="dtab")
+        tab = const.tile([P, 16, 2 * DH], BF16, name="tab")
 
         def load_w(eng, s, k, w):
             eng.dma_start(
@@ -75,20 +76,14 @@ def tile_dualmultiheadattention_pa_t_kernel(tc, x_1, x_2, cos1, sin1, cos2, sin2
                 in_=w.rearrange("(u q e) c -> q u (e c)", u=2, e=2),
             )
 
-        cos1v = cos1.rearrange("(p t) c -> p t c", t=12)
-        sin1v = sin1.rearrange("(p t) c -> p t c", t=12)
         load_x(0)
-        nc.scalar.dma_start(out=craw[:, 0:4, :], in_=cos1v[:, 0:4, :])
-        nc.scalar.dma_start(out=sraw[:, 0:4, :], in_=sin1v[:, 0:4, :])
         load_w(nc.scalar, 0, 0, wq1)
         load_w(nc.scalar, 0, 1, wk1)
         for r0, bvec in ((0, bq1), (2, bk1), (4, bq2), (6, bk2)):
             nc.sync.dma_start(out=brow[r0 : r0 + 2, :], in_=bvec.rearrange("(r m) -> r m", r=2))
-        for r in range(1, 4):
-            load_x(r)
-        nc.sync.dma_start(out=craw[:, 4:12, :], in_=cos1v[:, 4:12, :])
-        nc.sync.dma_start(out=sraw[:, 4:12, :], in_=sin1v[:, 4:12, :])
-        for r in range(4, 6):
+        nc.scalar.dma_start(out=craw[:, 0:12, :], in_=cos1.rearrange("(p t) c -> p t c", t=12))
+        nc.scalar.dma_start(out=sraw[:, 0:12, :], in_=sin1.rearrange("(p t) c -> p t c", t=12))
+        for r in range(1, 6):
             load_x(r)
         nc.sync.dma_start(out=craw[:, 12:16, :], in_=cos2.rearrange("(p t) c -> p t c", t=4))
         nc.sync.dma_start(out=sraw[:, 12:16, :], in_=sin2.rearrange("(p t) c -> p t c", t=4))
@@ -96,12 +91,6 @@ def tile_dualmultiheadattention_pa_t_kernel(tc, x_1, x_2, cos1, sin1, cos2, sin2
         load_w(nc.sync, 1, 1, wk2)
         for r in range(6, NR):
             load_x(r)
-
-        swp = const.tile([P, P], F32, name="swp")
-        swv = swp[:].rearrange("p (m e) -> p m e", e=2)
-        idv = ident[:].rearrange("p (m e) -> p m e", e=2)
-        nc.vector.tensor_copy(out=swv[:, :, 0], in_=idv[:, :, 1])
-        nc.vector.tensor_copy(out=swv[:, :, 1], in_=idv[:, :, 0])
 
         def regroup_w(copy, s, k):
             copy(
@@ -114,50 +103,43 @@ def tile_dualmultiheadattention_pa_t_kernel(tc, x_1, x_2, cos1, sin1, cos2, sin2
                 out=wcod[s][:].bitcast(FP8X4), scales=wscl[s][:], in_=wgrp[s][:].rearrange("p c t -> p (c t)")
             )
 
+        tabv = tab[:].rearrange("p t (j i e) -> p t j i e", i=2, e=2)
+        crv = craw[:].rearrange("p t (j e) -> p t j e", e=2)
         srv = sraw[:].rearrange("p t (j e) -> p t j e", e=2)
-        tabsrc = {}
 
-        def table_sources(eng, g):
+        def table_op(on_vector, g, k):
             tsl = slice(4 * g, 4 * g + 4)
-            csrc = spool.tile([P, 4, 2, DH], F32, name="csrc")
-            ssrc = spool.tile([P, 4, 2, DH], F32, name="ssrc")
-            eng.tensor_scalar(
-                out=csrc[:], in0=craw[:, tsl, :].unsqueeze(2).to_broadcast([P, 4, 2, DH]),
-                scalar1=1.0, scalar2=0.0, op0=ALU.mult, op1=ALU.add,
-            )
-            ssv = ssrc[:].rearrange("p t h (j e) -> p t h j e", e=2)
-            for e in range(2):
-                eng.tensor_scalar(
-                    out=ssv[:, :, :, :, e],
-                    in0=srv[:, tsl, :, 1 - e].unsqueeze(2).to_broadcast([P, 4, 2, DH // 2]),
-                    scalar1=(1.0 if e == 0 else -1.0), scalar2=0.0, op0=ALU.mult, op1=ALU.add,
-                )
-            tabsrc[g] = (csrc, ssrc)
-
-        def table_transpose(pool, name, g, z):
-            bank = pool.tile([P, 4, P], F32, name=name)
-            for t in range(4):
-                nc.tensor.transpose(bank[:, t, :], tabsrc[g][z][:, t].rearrange("p h c -> p (h c)"), ident[:])
-            nc.scalar.copy(out=dtab[:, z, 4 * g * P : 4 * (g + 1) * P], in_=bank[:].rearrange("p t n -> p (t n)"))
+            src, i, e, sign = ((crv, 0, 0, 1.0), (srv, 0, 1, -1.0), (srv, 1, 0, 1.0), (crv, 1, 1, 1.0))[k]
+            dst = tabv[:, tsl, :, i, e]
+            val = src[:, tsl, :, i]
+            if on_vector:
+                nc.vector.tensor_scalar_mul(out=dst, in0=val, scalar1=sign)
+            else:
+                nc.scalar.mul(out=dst, in_=val, mul=sign)
 
         grouped = {}
         xcod = {}
         xscl = {}
 
-        def transpose_x(r, half):
+        xts = {}
+
+        def transpose_x(r, tau):
             words = xs[r][:].bitcast(F32)
-            if half == 0:
+            if tau == 0:
                 grp = gpool.tile([P, 8 * P], F32, name="grp", align_bytes=64)
                 grouped[r] = grp
-            xt = ps_xt.tile([P, 2, 2, P], F32, name="xt")
-            for a in range(2):
-                for u in range(2):
-                    c0 = (2 * half + a) * 256 + u * P
-                    nc.tensor.transpose(xt[:, a, u, :], words[:, c0 : c0 + P], ident[:])
-            nc.scalar.copy(
-                out=grouped[r][:, half * 512 : (half + 1) * 512].rearrange("q (a p u) -> q a p u", a=2, u=2),
-                in_=xt[:].rearrange("q a u p -> q a p u"),
-            )
+            half, a = tau // 2, tau % 2
+            if a == 0:
+                xt = ps_xt.tile([P, 2, 2, P], F32, name="xt")
+                xts[r] = xt
+            for u in range(2):
+                c0 = tau * 256 + u * P
+                nc.tensor.transpose(xts[r][:, a, u, :], words[:, c0 : c0 + P], ident[:])
+            if a == 1:
+                nc.scalar.copy(
+                    out=grouped[r][:, half * 512 : (half + 1) * 512].rearrange("q (a p u) -> q a p u", a=2, u=2),
+                    in_=xts[r][:].rearrange("q a u p -> q a p u"),
+                )
 
         def quantise_x(r):
             cod = cpool.tile([P, 4 * P], U32, name="xcod", align_bytes=64)
@@ -166,100 +148,96 @@ def tile_dualmultiheadattention_pa_t_kernel(tc, x_1, x_2, cos1, sin1, cos2, sin2
             xcod[r] = cod
             xscl[r] = scl
 
-        banks = {}
+        proj = {}
 
-        def project(r):
+        def project(r, fb):
             s = ROUNDS[r][0]
-            for fb in range(4):
-                fsl = slice(fb * P, (fb + 1) * P)
-                p1 = ps_p1.tile([P, 4 * P], F32, name="p1")
-                nc.tensor.matmul_mx(
-                    out=p1[:],
-                    lhsT=wcod[s][:, fsl].bitcast(FP8X4),
-                    lhsT_scale=wscl[s][:, fsl],
-                    rhs=xcod[r][:].bitcast(FP8X4),
-                    rhs_scale=xscl[r][:],
-                    start=True,
-                    stop=True,
-                )
-                banks[(r, fb)] = p1
+            fsl = slice(fb * P, (fb + 1) * P)
+            p1 = ps_p1.tile([P, 4 * P], F32, name="p1")
+            nc.tensor.matmul_mx(
+                out=p1[:],
+                lhsT=wcod[s][:, fsl].bitcast(FP8X4),
+                lhsT_scale=wscl[s][:, fsl],
+                rhs=xcod[r][:].bitcast(FP8X4),
+                rhs_scale=xscl[r][:],
+                start=True,
+                stop=True,
+            )
+            t_sb = tpool.tile([P, 4 * P], F32, name="t_sb")
+            nc.scalar.activation(
+                out=t_sb[:],
+                in_=p1[:],
+                func=ACT.Identity,
+                bias=bias_p[:, 4 * s + fb : 4 * s + fb + 1],
+                scale=(0.125 if fb < 2 else 1.0),
+            )
+            proj[(r, fb)] = t_sb
 
-        table_sources(nc.vector, 0)
         regroup_w(nc.vector.tensor_copy, 0, 0)
         regroup_w(nc.vector.tensor_copy, 0, 1)
         quantise_w(0)
-        transpose_x(0, 0)
-        table_transpose(ps_p2, "p2", 0, 0)
-        transpose_x(0, 1)
-        table_transpose(ps_p2, "p2", 0, 1)
-        quantise_x(0)
-        transpose_x(1, 0)
-        transpose_x(1, 1)
-        project(0)
+        for tau in range(4):
+            transpose_x(0, tau)
         brow32 = const.tile([P, P], F32, name="brow32")
         nc.vector.tensor_copy(out=brow32[:], in_=brow[:])
-        bT = ps_p1.tile([P, 4 * P], F32, name="p1")
+        bT = ps_p2.tile([P, 4 * P], F32, name="p2")
         nc.tensor.transpose(bT[:, 0:P], brow32[:], ident[:])
+        quantise_x(0)
         bias_p = const.tile([P, 8], F32, name="bias_p")
-        nc.vector.tensor_copy(out=bias_p[:], in_=bT[:, 0:8])
-        transpose_x(2, 0)
-        transpose_x(2, 1)
+        bv = bias_p[:].rearrange("p (s k r) -> p s k r", s=2, k=2)
+        tv = bT[:, 0:8].rearrange("p (s k r) -> p s k r", s=2, k=2)
+        nc.vector.tensor_scalar_mul(out=bv[:, :, 0, :], in0=tv[:, :, 0, :], scalar1=0.125)
+        nc.vector.tensor_copy(out=bv[:, :, 1, :], in_=tv[:, :, 1, :])
+        for k in range(4):
+            table_op(True, 0, k)
+        for tau in range(4):
+            transpose_x(1, tau)
+        for fb in range(4):
+            project(0, fb)
+        quantise_x(1)
+        for tau in range(4):
+            transpose_x(2, tau)
 
         for r in range(NR):
             s, tg, b = ROUNDS[r]
             g = tg if s == 0 else 3
+            prod = rpool.tile([P, 4, 8 * P], F32, name="prod")
             y = ypool.tile([P, 2 * H, 4, DH], F32, name="y")
-            if r % 4 == 0 and r < 12:
-                table_sources(nc.gpsimd, r // 4 + 1)
-            for fb in range(4):
-                p1 = banks[(r, fb)]
-                bcol = bias_p[:, 4 * s + fb : 4 * s + fb + 1]
-                dsl = dtab[:, :, 4 * g * P : 4 * (g + 1) * P]
-                prod = rpool.tile([P, 2, 4 * P], F32, name="prod")
-                if (r % 1, fb) in POOL_BLOCKS:
-                    t_sb = tpool.tile([P, 4 * P], F32, name="t_sb")
-                    nc.scalar.activation(out=t_sb[:], in_=p1[:], func=ACT.Identity, bias=bcol, scale=1.0)
-                    nc.gpsimd.tensor_tensor(
-                        out=prod[:], in0=t_sb[:].unsqueeze(1).to_broadcast([P, 2, 4 * P]), in1=dsl, op=ALU.mult
+            for tau in range(4):
+                p2 = ps_p2.tile([P, 4 * P], F32, name="p2")
+                for fb in range(4):
+                    nc.tensor.transpose(
+                        p2[:, fb * P : (fb + 1) * P], proj[(r, fb)][:, tau * P : (tau + 1) * P], ident[:]
                     )
-                else:
-                    nc.vector.scalar_tensor_tensor(
-                        out=prod[:],
-                        in0=p1[:].unsqueeze(1).to_broadcast([P, 2, 4 * P]),
-                        scalar=bcol,
-                        in1=dsl,
-                        op0=ALU.add,
-                        op1=ALU.mult,
-                    )
-                if r == 0 and fb == 1:
-                    quantise_x(1)
-                p2 = ps_p2.tile([P, 4, P], F32, name="p2")
-                for tau in range(4):
-                    tsl = slice(tau * P, (tau + 1) * P)
-                    nc.tensor.matmul(
-                        out=p2[:, tau, :], lhsT=prod[:, 0, tsl], rhs=ident[:], is_transpose=True, start=True, stop=False
-                    )
-                    nc.tensor.matmul(
-                        out=p2[:, tau, :], lhsT=prod[:, 1, tsl], rhs=swp[:], is_transpose=True, start=False, stop=True
-                    )
-                nc.scalar.mul(
-                    out=y[:, 2 * fb : 2 * fb + 2],
-                    in_=p2[:].rearrange("p t (h c) -> p h t c", h=2),
-                    mul=(0.125 if fb < 2 else 1.0),
+                if r + 3 < NR:
+                    transpose_x(r + 3, tau)
+                if r + 1 < NR:
+                    project(r + 1, tau)
+                if tau == 1 and r < 12:
+                    table_op(False, r // 4 + 1, r % 4)
+                if tau == 3 and r in (4, 5):
+                    regroup_w(nc.scalar.copy, 1, r - 4)
+                nc.vector.tensor_tensor(
+                    out=prod[:, tau, :].rearrange("p (g j i e) -> p g j i e", g=8, i=2, e=2),
+                    in0=p2[:].rearrange("p (g j e) -> p g j e", g=8, e=2).unsqueeze(3).to_broadcast([P, 8, 32, 2, 2]),
+                    in1=tab[:, 4 * g + tau, :]
+                    .rearrange("p (j i e) -> p j i e", i=2, e=2)
+                    .unsqueeze(1)
+                    .to_broadcast([P, 8, 32, 2, 2]),
+                    op=ALU.mult,
                 )
-                if fb < 2 and r + 3 < NR:
-                    transpose_x(r + 3, fb)
-                if fb == 1:
-                    nc.sync.dma_start(out=out_view(out_0, r), in_=y[:, 0:H])
-                if fb == 2:
-                    if r % 4 in (1, 2) and r < 12:
-                        table_transpose(ps_xt, "xt", r // 4 + 1, r % 4 - 1)
-                    if r in (4, 5):
-                        regroup_w(nc.scalar.copy, 1, r - 4)
-                    if r + 1 < NR:
-                        project(r + 1)
-            if r + 2 < NR:
-                quantise_x(r + 2)
-            if r == 7:
-                quantise_w(1)
+                if tau == 0 and r + 2 < NR:
+                    quantise_x(r + 2)
+                if tau == 2 and r == 7:
+                    quantise_w(1)
+                if tau % GT == GT - 1:
+                    t0 = tau - GT + 1
+                    pv = prod[:, t0 : tau + 1, :].rearrange("p t (g c e) -> p t g c e", g=8, e=2)
+                    nc.gpsimd.tensor_tensor(
+                        out=y[:].rearrange("p g t c -> p t g c")[:, t0 : tau + 1],
+                        in0=pv[:, :, :, :, 0],
+                        in1=pv[:, :, :, :, 1],
+                        op=ALU.add,
+                    )
+            nc.sync.dma_start(out=out_view(out_0, r), in_=y[:, 0:H])
             nc.sync.dma_start(out=out_view(out_1, r), in_=y[:, H : 2 * H])

@@ -36,7 +36,9 @@ def tile_dualmultiheadattention_pa_t_kernel(tc, x_1, x_2, cos1, sin1, cos2, sin2
         ypool = ctx.enter_context(tc.tile_pool(name="res", bufs=3))
         ps_xt = ctx.enter_context(tc.psum_pool(name="ps_xt", bufs=2))
         ps_p1 = ctx.enter_context(tc.psum_pool(name="ps_p1", bufs=2))
-        ps_p2 = ctx.enter_context(tc.psum_pool(name="ps_p2", bufs=4))
+        ps_p2 = ctx.enter_context(tc.psum_pool(name="ps_p2", bufs=3))
+
+        ps_fill = ctx.enter_context(tc.psum_pool(name="ps_fill", bufs=1))
 
         def x_view(r):
             s, tg, b = ROUNDS[r]
@@ -173,6 +175,21 @@ def tile_dualmultiheadattention_pa_t_kernel(tc, x_1, x_2, cos1, sin1, cos2, sin2
             )
             proj[(r, fb)] = t_sb
 
+        fill = ps_fill.tile([P, 4 * P], F32, name="fill")
+
+        def filler(r, n):
+            s = ROUNDS[r][0]
+            for q in range(n):
+                nc.tensor.matmul_mx(
+                    out=fill[:],
+                    lhsT=wcod[s][:, 0:P].bitcast(FP8X4),
+                    lhsT_scale=wscl[s][:, 0:P],
+                    rhs=xcod[r][:].bitcast(FP8X4),
+                    rhs_scale=xscl[r][:],
+                    start=True,
+                    stop=True,
+                )
+
         regroup_w(nc.vector.tensor_copy, 0, 0)
         regroup_w(nc.vector.tensor_copy, 0, 1)
         quantise_w(0)
@@ -203,41 +220,50 @@ def tile_dualmultiheadattention_pa_t_kernel(tc, x_1, x_2, cos1, sin1, cos2, sin2
             g = tg if s == 0 else 3
             prod = rpool.tile([P, 4, 8 * P], F32, name="prod")
             y = ypool.tile([P, 2 * H, 4, DH], F32, name="y")
-            for tau in range(4):
-                p2 = ps_p2.tile([P, 4 * P], F32, name="p2")
-                for fb in range(4):
-                    nc.tensor.transpose(
-                        p2[:, fb * P : (fb + 1) * P], proj[(r, fb)][:, tau * P : (tau + 1) * P], ident[:]
-                    )
+            for half in range(2):
+                taus = (2 * half, 2 * half + 1)
                 if r + 3 < NR:
-                    transpose_x(r + 3, tau)
+                    for tau in taus:
+                        transpose_x(r + 3, tau)
+                p2s = {}
+                for tau in taus:
+                    p2 = ps_p2.tile([P, 4 * P], F32, name="p2")
+                    for fb in range(4):
+                        nc.tensor.transpose(
+                            p2[:, fb * P : (fb + 1) * P], proj[(r, fb)][:, tau * P : (tau + 1) * P], ident[:]
+                        )
+                    p2s[tau] = p2
                 if r + 1 < NR:
-                    project(r + 1, tau)
-                if tau == 1 and r < 12:
+                    for tau in taus:
+                        project(r + 1, tau)
+                filler(min(r + 1, NR - 1), 2)
+                if half == 0 and r < 12:
                     table_op(False, r // 4 + 1, r % 4)
-                if tau == 3 and r in (4, 5):
+                if half == 1 and r in (4, 5):
                     regroup_w(nc.scalar.copy, 1, r - 4)
-                nc.vector.tensor_tensor(
-                    out=prod[:, tau, :].rearrange("p (g j i e) -> p g j i e", g=8, i=2, e=2),
-                    in0=p2[:].rearrange("p (g j e) -> p g j e", g=8, e=2).unsqueeze(3).to_broadcast([P, 8, 32, 2, 2]),
-                    in1=tab[:, 4 * g + tau, :]
-                    .rearrange("p (j i e) -> p j i e", i=2, e=2)
-                    .unsqueeze(1)
-                    .to_broadcast([P, 8, 32, 2, 2]),
-                    op=ALU.mult,
-                )
-                if tau == 0 and r + 2 < NR:
-                    quantise_x(r + 2)
-                if tau == 2 and r == 7:
-                    quantise_w(1)
-                if tau % GT == GT - 1:
-                    t0 = tau - GT + 1
-                    pv = prod[:, t0 : tau + 1, :].rearrange("p t (g c e) -> p t g c e", g=8, e=2)
-                    nc.gpsimd.tensor_tensor(
-                        out=y[:].rearrange("p g t c -> p t g c")[:, t0 : tau + 1],
-                        in0=pv[:, :, :, :, 0],
-                        in1=pv[:, :, :, :, 1],
-                        op=ALU.add,
+                for tau in taus:
+                    nc.vector.tensor_tensor(
+                        out=prod[:, tau, :].rearrange("p (g j i e) -> p g j i e", g=8, i=2, e=2),
+                        in0=p2s[tau][:]
+                        .rearrange("p (g j e) -> p g j e", g=8, e=2)
+                        .unsqueeze(3)
+                        .to_broadcast([P, 8, 32, 2, 2]),
+                        in1=tab[:, 4 * g + tau, :]
+                        .rearrange("p (j i e) -> p j i e", i=2, e=2)
+                        .unsqueeze(1)
+                        .to_broadcast([P, 8, 32, 2, 2]),
+                        op=ALU.mult,
                     )
+                    if tau == 0 and r + 2 < NR:
+                        quantise_x(r + 2)
+                    if tau == 2 and r == 7:
+                        quantise_w(1)
+                pv = prod[:, taus[0] : taus[1] + 1, :].rearrange("p t (g c e) -> p t g c e", g=8, e=2)
+                nc.gpsimd.tensor_tensor(
+                    out=y[:].rearrange("p g t c -> p t g c")[:, taus[0] : taus[1] + 1],
+                    in0=pv[:, :, :, :, 0],
+                    in1=pv[:, :, :, :, 1],
+                    op=ALU.add,
+                )
             nc.sync.dma_start(out=out_view(out_0, r), in_=y[:, 0:H])
             nc.sync.dma_start(out=out_view(out_1, r), in_=y[:, H : 2 * H])

@@ -36,9 +36,7 @@ def tile_dualmultiheadattention_pa_t_kernel(tc, x_1, x_2, cos1, sin1, cos2, sin2
         ypool = ctx.enter_context(tc.tile_pool(name="res", bufs=3))
         ps_xt = ctx.enter_context(tc.psum_pool(name="ps_xt", bufs=2))
         ps_p1 = ctx.enter_context(tc.psum_pool(name="ps_p1", bufs=2))
-        ps_p2 = ctx.enter_context(tc.psum_pool(name="ps_p2", bufs=3))
-
-        ps_fill = ctx.enter_context(tc.psum_pool(name="ps_fill", bufs=1))
+        ps_p2 = ctx.enter_context(tc.psum_pool(name="ps_p2", bufs=4))
 
         def x_view(r):
             s, tg, b = ROUNDS[r]
@@ -175,21 +173,6 @@ def tile_dualmultiheadattention_pa_t_kernel(tc, x_1, x_2, cos1, sin1, cos2, sin2
             )
             proj[(r, fb)] = t_sb
 
-        fill = ps_fill.tile([P, 4 * P], F32, name="fill")
-
-        def filler(r, n):
-            s = ROUNDS[r][0]
-            for q in range(n):
-                nc.tensor.matmul_mx(
-                    out=fill[:],
-                    lhsT=wcod[s][:, 0:P].bitcast(FP8X4),
-                    lhsT_scale=wscl[s][:, 0:P],
-                    rhs=xcod[r][:].bitcast(FP8X4),
-                    rhs_scale=xscl[r][:],
-                    start=True,
-                    stop=True,
-                )
-
         regroup_w(nc.vector.tensor_copy, 0, 0)
         regroup_w(nc.vector.tensor_copy, 0, 1)
         quantise_w(0)
@@ -220,50 +203,67 @@ def tile_dualmultiheadattention_pa_t_kernel(tc, x_1, x_2, cos1, sin1, cos2, sin2
             g = tg if s == 0 else 3
             prod = rpool.tile([P, 4, 8 * P], F32, name="prod")
             y = ypool.tile([P, 2 * H, 4, DH], F32, name="y")
-            for half in range(2):
-                taus = (2 * half, 2 * half + 1)
-                if r + 3 < NR:
-                    for tau in taus:
-                        transpose_x(r + 3, tau)
-                p2s = {}
-                for tau in taus:
-                    p2 = ps_p2.tile([P, 4 * P], F32, name="p2")
-                    for fb in range(4):
-                        nc.tensor.transpose(
-                            p2[:, fb * P : (fb + 1) * P], proj[(r, fb)][:, tau * P : (tau + 1) * P], ident[:]
-                        )
-                    p2s[tau] = p2
-                if r + 1 < NR:
-                    for tau in taus:
-                        project(r + 1, tau)
-                filler(min(r + 1, NR - 1), 2)
-                if half == 0 and r < 12:
-                    table_op(False, r // 4 + 1, r % 4)
-                if half == 1 and r in (4, 5):
-                    regroup_w(nc.scalar.copy, 1, r - 4)
-                for tau in taus:
-                    nc.vector.tensor_tensor(
-                        out=prod[:, tau, :].rearrange("p (g j i e) -> p g j i e", g=8, i=2, e=2),
-                        in0=p2s[tau][:]
-                        .rearrange("p (g j e) -> p g j e", g=8, e=2)
-                        .unsqueeze(3)
-                        .to_broadcast([P, 8, 32, 2, 2]),
-                        in1=tab[:, 4 * g + tau, :]
-                        .rearrange("p (j i e) -> p j i e", i=2, e=2)
-                        .unsqueeze(1)
-                        .to_broadcast([P, 8, 32, 2, 2]),
-                        op=ALU.mult,
+            p2s = []
+
+            def back(tau):
+                p2 = ps_p2.tile([P, 4 * P], F32, name="p2")
+                for fb in range(4):
+                    nc.tensor.transpose(
+                        p2[:, fb * P : (fb + 1) * P], proj[(r, fb)][:, tau * P : (tau + 1) * P], ident[:]
                     )
-                    if tau == 0 and r + 2 < NR:
-                        quantise_x(r + 2)
-                    if tau == 2 and r == 7:
-                        quantise_w(1)
-                pv = prod[:, taus[0] : taus[1] + 1, :].rearrange("p t (g c e) -> p t g c e", g=8, e=2)
-                nc.gpsimd.tensor_tensor(
-                    out=y[:].rearrange("p g t c -> p t g c")[:, taus[0] : taus[1] + 1],
+                p2s.append(p2)
+
+            def pair_sum(eng, t0, t1):
+                pv = prod[:, t0:t1, :].rearrange("p t (g c e) -> p t g c e", g=8, e=2)
+                eng.tensor_tensor(
+                    out=y[:].rearrange("p g t c -> p t g c")[:, t0:t1],
                     in0=pv[:, :, :, :, 0],
                     in1=pv[:, :, :, :, 1],
                     op=ALU.add,
                 )
-            nc.sync.dma_start(out=out_view(out_0, r), in_=y[:, 0:H])
-            nc.sync.dma_start(out=out_view(out_1, r), in_=y[:, H : 2 * H])
+
+            for tau in range(3):
+                back(tau)
+            if r + 1 < NR:
+                for fb in range(4):
+                    project(r + 1, fb)
+            if r + 3 < NR:
+                for tau in range(4):
+                    transpose_x(r + 3, tau)
+            if r < 12:
+                table_op(False, r // 4 + 1, r % 4)
+            if r in (4, 5):
+                regroup_w(nc.scalar.copy, 1, r - 4)
+            for tau in range(3, 4):
+                back(tau)
+            last = r == NR - 1
+            for tau in range(4):
+                nc.vector.tensor_tensor(
+                    out=prod[:, tau, :].rearrange("p (g j i e) -> p g j i e", g=8, i=2, e=2),
+                    in0=p2s[tau][:].rearrange("p (g j e) -> p g j e", g=8, e=2).unsqueeze(3).to_broadcast([P, 8, 32, 2, 2]),
+                    in1=tab[:, 4 * g + tau, :]
+                    .rearrange("p (j i e) -> p j i e", i=2, e=2)
+                    .unsqueeze(1)
+                    .to_broadcast([P, 8, 32, 2, 2]),
+                    op=ALU.mult,
+                )
+                if tau == 0 and r + 2 < NR:
+                    quantise_x(r + 2)
+                if tau == 2 and r == 7:
+                    quantise_w(1)
+                if tau == 1:
+                    pair_sum(nc.gpsimd, 0, 2)
+                    if last:
+                        nc.sync.dma_start(out=out_view(out_0, r)[:, :, 0:2, :], in_=y[:, 0:H, 0:2, :])
+                        nc.sync.dma_start(out=out_view(out_1, r)[:, :, 0:2, :], in_=y[:, H : 2 * H, 0:2, :])
+                if tau == 2 and last:
+                    pair_sum(nc.gpsimd, 2, 3)
+                if tau == 3:
+                    if last:
+                        pair_sum(nc.vector, 3, 4)
+                        nc.sync.dma_start(out=out_view(out_0, r)[:, :, 2:4, :], in_=y[:, 0:H, 2:4, :])
+                        nc.scalar.dma_start(out=out_view(out_1, r)[:, :, 2:4, :], in_=y[:, H : 2 * H, 2:4, :])
+                    else:
+                        pair_sum(nc.gpsimd, 2, 4)
+                        nc.sync.dma_start(out=out_view(out_0, r), in_=y[:, 0:H])
+                        nc.sync.dma_start(out=out_view(out_1, r), in_=y[:, H : 2 * H])

@@ -247,11 +247,11 @@ def tile_dualmultiheadattention_pa_t_kernel(tc, x_1, x_2, cos1, sin1, cos2, sin2
                     .to_broadcast([P, 8, 32, 2, 2]),
                     op=ALU.mult,
                 )
-                if tau == 0 and r + 2 < NR:
-                    quantise_x(r + 2)
-                if tau == 2 and r == 7:
-                    quantise_w(1)
                 if tau == 1:
+                    if r + 2 < NR:
+                        quantise_x(r + 2)
+                    if r == 7:
+                        quantise_w(1)
                     pair_sum(nc.gpsimd, 0, 2)
                     if last:
                         nc.sync.dma_start(out=out_view(out_0, r)[:, :, 0:2, :], in_=y[:, 0:H, 0:2, :])

from contextlib import ExitStack

import concourse.mybir as mybir
from concourse.masks import make_identity

F32 = mybir.dt.float32
BF16 = mybir.dt.bfloat16
U32 = mybir.dt.uint32
U8 = mybir.dt.uint8
FP8X4 = mybir.dt.float8_e4m3fn_x4
ALU = mybir.AluOpType
ACT = mybir.ActivationFunctionType

P = 128
B, N1, N2, D, H, DH = 4, 1536, 512, 512, 4, 64
E = H * DH
FLOPS = 2 * B * (N1 + N2) * D * 2 * E

ROUNDS = [(0, tg, b) for tg in range(3) for b in range(B)] + [(1, 0, b) for b in range(B)]
NR = len(ROUNDS)
MANUAL = True
GT = 2


def tile_dualmultiheadattention_pa_t_kernel(tc, x_1, x_2, cos1, sin1, cos2, sin2, wq1, bq1, wk1, bk1, wq2, bq2, wk2, bk2, out_0, out_1):
    nc = tc.nc
    with ExitStack() as ctx:
        if MANUAL:
            ctx.enter_context(tc.manual_schedule())
        const = ctx.enter_context(tc.tile_pool(name="const", bufs=1))
        xpool = ctx.enter_context(tc.tile_pool(name="xin", bufs=NR))
        gpool = ctx.enter_context(tc.tile_pool(name="grouped", bufs=3))
        cpool = ctx.enter_context(tc.tile_pool(name="codes", bufs=3))
        tpool = ctx.enter_context(tc.tile_pool(name="proj", bufs=8))
        rpool = ctx.enter_context(tc.tile_pool(name="prod", bufs=2))
        ypool = ctx.enter_context(tc.tile_pool(name="res", bufs=3))
        ps_xt = ctx.enter_context(tc.psum_pool(name="ps_xt", bufs=2))
        ps_p1 = ctx.enter_context(tc.psum_pool(name="ps_p1", bufs=2))
        ps_p2 = ctx.enter_context(tc.psum_pool(name="ps_p2", bufs=4))

        def x_view(r):
            s, tg, b = ROUNDS[r]
            if s == 0:
                return x_1[b].rearrange("(p t) k -> p t k", t=12)[:, 4 * tg : 4 * tg + 4, :]
            return x_2[b].rearrange("(p t) k -> p t k", t=4)

        def out_view(o, r):
            s, tg, b = ROUNDS[r]
            if s == 0:
                return o[b, :, 0:N1, :].rearrange("h (p t) c -> p h t c", t=12)[:, :, 4 * tg : 4 * tg + 4, :]
            return o[b, :, N1 : N1 + N2, :].rearrange("h (p t) c -> p h t c", t=4)

        xs = []

        def load_x(r):
            x_sb = xpool.tile([P, 4 * D], BF16, name="x_sb")
            nc.sync.dma_start(out=x_sb[:].rearrange("p (t k) -> p t k", t=4), in_=x_view(r))
            xs.append(x_sb)

        ident = const.tile([P, P], F32, name="ident")
        make_identity(nc, ident[:])
        brow = const.tile([P, P], BF16, name="brow")
        nc.vector.memset(brow[:], 0.0)

        wraw = [const.tile([P, 2, 4, E], BF16, name="wraw%d" % s) for s in range(2)]
        wgrp = [const.tile([P, 2 * E, 4], BF16, name="wgrp%d" % s, align_bytes=64) for s in range(2)]
        wcod = [const.tile([P, 2 * E], U32, name="wcod%d" % s, align_bytes=64) for s in range(2)]
        wscl = [const.tile([P, 2 * E], U8, name="wscl%d" % s, align_bytes=64) for s in range(2)]
        craw = const.tile([P, 16, DH], BF16, name="craw")
        sraw = const.tile([P, 16, DH], BF16, name="sraw")
        tab = const.tile([P, 16, 2 * DH], BF16, name="tab")

        def load_w(eng, s, k, w):
            eng.dma_start(
                out=wraw[s][:, k].rearrange("q (u e) c -> q u (e c)", u=2),
                in_=w.rearrange("(u q e) c -> q u (e c)", u=2, e=2),
            )

        load_x(0)
        load_w(nc.scalar, 0, 0, wq1)
        load_w(nc.scalar, 0, 1, wk1)
        for r0, bvec in ((0, bq1), (2, bk1), (4, bq2), (6, bk2)):
            nc.sync.dma_start(out=brow[r0 : r0 + 2, :], in_=bvec.rearrange("(r m) -> r m", r=2))
        nc.scalar.dma_start(out=craw[:, 0:12, :], in_=cos1.rearrange("(p t) c -> p t c", t=12))
        nc.scalar.dma_start(out=sraw[:, 0:12, :], in_=sin1.rearrange("(p t) c -> p t c", t=12))
        for r in range(1, 6):
            load_x(r)
        nc.sync.dma_start(out=craw[:, 12:16, :], in_=cos2.rearrange("(p t) c -> p t c", t=4))
        nc.sync.dma_start(out=sraw[:, 12:16, :], in_=sin2.rearrange("(p t) c -> p t c", t=4))
        load_w(nc.sync, 1, 0, wq2)
        load_w(nc.sync, 1, 1, wk2)
        for r in range(6, NR):
            load_x(r)

        def regroup_w(copy, s, k):
            copy(
                out=wgrp[s][:, k * E : (k + 1) * E, :].rearrange("p (c i) t -> p c t i", i=4),
                in_=wraw[s][:, k].rearrange("p t (c i) -> p c t i", i=4),
            )

        def quantise_w(s):
            nc.vector.quantize_mx(
                out=wcod[s][:].bitcast(FP8X4), scales=wscl[s][:], in_=wgrp[s][:].rearrange("p c t -> p (c t)")
            )

        tabv = tab[:].rearrange("p t (j i e) -> p t j i e", i=2, e=2)
        crv = craw[:].rearrange("p t (j e) -> p t j e", e=2)
        srv = sraw[:].rearrange("p t (j e) -> p t j e", e=2)

        def table_op(on_vector, g, k):
            tsl = slice(4 * g, 4 * g + 4)
            src, i, e, sign = ((crv, 0, 0, 1.0), (srv, 0, 1, -1.0), (srv, 1, 0, 1.0), (crv, 1, 1, 1.0))[k]
            dst = tabv[:, tsl, :, i, e]
            val = src[:, tsl, :, i]
            if on_vector:
                nc.vector.tensor_scalar_mul(out=dst, in0=val, scalar1=sign)
            else:
                nc.scalar.mul(out=dst, in_=val, mul=sign)

        grouped = {}
        xcod = {}
        xscl = {}

        xts = {}

        def transpose_x(r, tau):
            words = xs[r][:].bitcast(F32)
            if tau == 0:
                grp = gpool.tile([P, 8 * P], F32, name="grp", align_bytes=64)
                grouped[r] = grp
            half, a = tau // 2, tau % 2
            if a == 0:
                xt = ps_xt.tile([P, 2, 2, P], F32, name="xt")
                xts[r] = xt
            for u in range(2):
                c0 = tau * 256 + u * P
                nc.tensor.transpose(xts[r][:, a, u, :], words[:, c0 : c0 + P], ident[:])
            if a == 1:
                nc.scalar.copy(
                    out=grouped[r][:, half * 512 : (half + 1) * 512].rearrange("q (a p u) -> q a p u", a=2, u=2),
                    in_=xts[r][:].rearrange("q a u p -> q a p u"),
                )

        def quantise_x(r):
            cod = cpool.tile([P, 4 * P], U32, name="xcod", align_bytes=64)
            scl = cpool.tile([P, 4 * P], U8, name="xscl", align_bytes=64)
            nc.vector.quantize_mx(out=cod[:].bitcast(FP8X4), scales=scl[:], in_=grouped[r][:].bitcast(BF16))
            xcod[r] = cod
            xscl[r] = scl

        proj = {}

        def project(r, fb):
            s = ROUNDS[r][0]
            fsl = slice(fb * P, (fb + 1) * P)
            p1 = ps_p1.tile([P, 4 * P], F32, name="p1")
            nc.tensor.matmul_mx(
                out=p1[:],
                lhsT=wcod[s][:, fsl].bitcast(FP8X4),
                lhsT_scale=wscl[s][:, fsl],
                rhs=xcod[r][:].bitcast(FP8X4),
                rhs_scale=xscl[r][:],
                start=True,
                stop=True,
            )
            t_sb = tpool.tile([P, 4 * P], F32, name="t_sb")
            nc.scalar.activation(
                out=t_sb[:],
                in_=p1[:],
                func=ACT.Identity,
                bias=bias_p[:, 4 * s + fb : 4 * s + fb + 1],
                scale=(0.125 if fb < 2 else 1.0),
            )
            proj[(r, fb)] = t_sb

        regroup_w(nc.vector.tensor_copy, 0, 0)
        regroup_w(nc.vector.tensor_copy, 0, 1)
        quantise_w(0)
        for tau in range(4):
            transpose_x(0, tau)
        brow32 = const.tile([P, P], F32, name="brow32")
        nc.vector.tensor_copy(out=brow32[:], in_=brow[:])
        bT = ps_p2.tile([P, 4 * P], F32, name="p2")
        nc.tensor.transpose(bT[:, 0:P], brow32[:], ident[:])
        quantise_x(0)
        bias_p = const.tile([P, 8], F32, name="bias_p")
        bv = bias_p[:].rearrange("p (s k r) -> p s k r", s=2, k=2)
        tv = bT[:, 0:8].rearrange("p (s k r) -> p s k r", s=2, k=2)
        nc.vector.tensor_scalar_mul(out=bv[:, :, 0, :], in0=tv[:, :, 0, :], scalar1=0.125)
        nc.vector.tensor_copy(out=bv[:, :, 1, :], in_=tv[:, :, 1, :])
        for k in range(4):
            table_op(True, 0, k)
        for tau in range(4):
            transpose_x(1, tau)
        for fb in range(4):
            project(0, fb)
        quantise_x(1)
        for tau in range(4):
            transpose_x(2, tau)

        for r in range(NR):
            s, tg, b = ROUNDS[r]
            g = tg if s == 0 else 3
            prod = rpool.tile([P, 4, 8 * P], F32, name="prod")
            y = ypool.tile([P, 2 * H, 4, DH], F32, name="y")
            p2s = []

            def back(tau):
                p2 = ps_p2.tile([P, 4 * P], F32, name="p2")
                for fb in range(4):
                    nc.tensor.transpose(
                        p2[:, fb * P : (fb + 1) * P], proj[(r, fb)][:, tau * P : (tau + 1) * P], ident[:]
                    )
                p2s.append(p2)

            def pair_sum(eng, t0, t1):
                pv = prod[:, t0:t1, :].rearrange("p t (g c e) -> p t g c e", g=8, e=2)
                eng.tensor_tensor(
                    out=y[:].rearrange("p g t c -> p t g c")[:, t0:t1],
                    in0=pv[:, :, :, :, 0],
                    in1=pv[:, :, :, :, 1],
                    op=ALU.add,
                )

            for tau in range(3):
                back(tau)
            if r + 1 < NR:
                for fb in range(4):
                    project(r + 1, fb)
            if r + 3 < NR:
                for tau in range(4):
                    transpose_x(r + 3, tau)
            if r < 12:
                table_op(False, r // 4 + 1, r % 4)
            if r in (4, 5):
                regroup_w(nc.scalar.copy, 1, r - 4)
            for tau in range(3, 4):
                back(tau)
            last = r == NR - 1
            for tau in range(4):
                nc.vector.tensor_tensor(
                    out=prod[:, tau, :].rearrange("p (g j i e) -> p g j i e", g=8, i=2, e=2),
                    in0=p2s[tau][:].rearrange("p (g j e) -> p g j e", g=8, e=2).unsqueeze(3).to_broadcast([P, 8, 32, 2, 2]),
                    in1=tab[:, 4 * g + tau, :]
                    .rearrange("p (j i e) -> p j i e", i=2, e=2)
                    .unsqueeze(1)
                    .to_broadcast([P, 8, 32, 2, 2]),
                    op=ALU.mult,
                )
                if tau == 1:
                    if r + 2 < NR:
                        quantise_x(r + 2)
                    if r == 7:
                        quantise_w(1)
                    pair_sum(nc.gpsimd, 0, 2)
                    if last:
                        nc.sync.dma_start(out=out_view(out_0, r)[:, :, 0:2, :], in_=y[:, 0:H, 0:2, :])
                        nc.sync.dma_start(out=out_view(out_1, r)[:, :, 0:2, :], in_=y[:, H : 2 * H, 0:2, :])
                if tau == 2 and last:
                    pair_sum(nc.gpsimd, 2, 3)
                if tau == 3:
                    if last:
                        pair_sum(nc.vector, 3, 4)
                        nc.sync.dma_start(out=out_view(out_0, r)[:, :, 2:4, :], in_=y[:, 0:H, 2:4, :])
                        nc.scalar.dma_start(out=out_view(out_1, r)[:, :, 2:4, :], in_=y[:, H : 2 * H, 2:4, :])
                    else:
                        pair_sum(nc.gpsimd, 2, 4)
                        nc.sync.dma_start(out=out_view(out_0, r), in_=y[:, 0:H])
                        nc.sync.dma_start(out=out_view(out_1, r), in_=y[:, H : 2 * H])
